import numpy as np
import ml_dtypes


def mxq(x, axis, fmt="e4m3"):
    dtype, down = {"e4m3": (ml_dtypes.float8_e4m3fn, 7), "e5m2": (ml_dtypes.float8_e5m2, 14)}[fmt]
    v = np.moveaxis(np.asarray(x, np.float32).astype(ml_dtypes.bfloat16).astype(np.float64), axis, -1)
    blocks = v.reshape(v.shape[:-1] + (-1, 32))
    amax = np.abs(blocks).max(-1, keepdims=True)
    byte = np.maximum(np.where(amax > 0, np.frexp(amax)[1] - 1 + 127, 0) - down, 1)
    scale = np.exp2(byte - 127.0)
    codes = (blocks / scale).astype(np.float32).astype(dtype).astype(np.float64)
    return np.moveaxis((codes * scale).reshape(v.shape), -1, axis)


WIDE = False


def mx_kscale(k):
    if not WIDE:
        return np.ones(k)
    levels = np.array([10, -10, 5, -5, 0])
    a = np.random.permutation(np.resize(levels, k // 512 * 4)).reshape(k // 512, 4)
    idx = np.arange(k)
    return np.exp2(a[idx // 512, idx % 128 // 32])


BF16 = ml_dtypes.bfloat16


def bf(x):
    return np.asarray(x, np.float32).astype(BF16)


def f64(x):
    return np.asarray(x).astype(np.float64)


T, B, D, H, HD, A = 512, 8, 512, 4, 128, 128
HH = H * HD
CAT = HH + D
EPS = 1e-5
AO = 0.6


def layer_norm(x, w, b):
    mu = x.mean(-1, keepdims=True)
    var = np.square(x - mu).mean(-1, keepdims=True)
    return (x - mu) * (1.0 / np.sqrt(var + EPS)) * w + b


def setup_inputs():
    t = mx_kscale(HH)
    w_out = np.random.standard_normal((CAT, D)) / np.sqrt(CAT)
    w_out[:HH] = w_out[:HH] / t[:, None]
    return {"u": bf(np.random.standard_normal((T, B, HH)) * t),
            "attn_out": bf(AO * np.random.standard_normal((T, B, HH)) * t),
            "src_norm": bf(np.random.standard_normal((T, B, D))),
            "w_out": bf(w_out),
            "b_out": bf(0.1 * np.random.standard_normal(D)),
            "ln2_w": bf(1.0 + 0.1 * np.random.standard_normal(D)),
            "ln2_b": bf(0.1 * np.random.standard_normal(D))}


def reference(u, attn_out, src_norm, w_out, b_out, ln2_w, ln2_b):
    residual = f64(u) + f64(attn_out)
    xn = f64(src_norm)
    cat = np.concatenate([residual, xn], -1)
    z = (mxq(cat, 2, "e4m3") @ mxq(f64(w_out), 0, "e4m3")) + f64(b_out)
    return layer_norm(z, f64(ln2_w), f64(ln2_b)) + xn

@@ -1,0 +1,167 @@
+from contextlib import ExitStack
+
+import concourse.mybir as mybir
+from concourse.masks import make_identity
+
+F32 = mybir.dt.float32
+BF16 = mybir.dt.bfloat16
+U32 = mybir.dt.uint32
+U8 = mybir.dt.uint8
+FP8X4 = mybir.dt.float8_e4m3fn_x4
+ALU = mybir.AluOpType
+ACT = mybir.ActivationFunctionType
+
+P = 128
+ROWS = 512 * 8
+D = 512
+PASSES = 2
+HALVES = 2
+GROUP_TILES = 4
+GROUP_ROWS = GROUP_TILES * P
+GROUPS = ROWS // GROUP_ROWS
+PAIR = 2
+EPS = 1e-5
+
+FLOPS = 2 * ROWS * (PASSES * 512) * D
+
+
+def tile_stulayer_pb_t_kernel(tc, u, attn_out, src_norm, w_out, b_out, ln2_w, ln2_b, out):
+    nc = tc.nc
+
+    def group_rows(x, g):
+        rows = x.flatten_outer_dims()[g * GROUP_ROWS : (g + 1) * GROUP_ROWS, :]
+        return rows.rearrange("(p n) d -> p (n d)", n=GROUP_TILES)
+
+    with ExitStack() as pools:
+        const = pools.enter_context(tc.tile_pool(name="const", bufs=1))
+        inputs = pools.enter_context(tc.tile_pool(name="inputs", bufs=1))
+        per_group = pools.enter_context(tc.tile_pool(name="per_group", bufs=2))
+        per_pair = pools.enter_context(tc.tile_pool(name="per_pair", bufs=3))
+        per_tile = pools.enter_context(tc.tile_pool(name="per_tile", bufs=4))
+        psum_t = pools.enter_context(tc.psum_pool(name="psum_t", bufs=4))
+        psum_z = pools.enter_context(tc.psum_pool(name="psum_z", bufs=4))
+
+        w_raw = const.tile([P, PASSES * HALVES, 2 * D], BF16)
+        nc.scalar.dma_start(
+            out=w_raw[:],
+            in_=w_out.rearrange("(s q e) n -> q s (e n)", s=PASSES * HALVES, e=2),
+        )
+        b_bc = const.tile([P, D], BF16)
+        nc.scalar.dma_start(out=b_bc[:], in_=b_out.partition_broadcast(P))
+        gain_bc = const.tile([P, D], BF16)
+        nc.scalar.dma_start(out=gain_bc[:], in_=ln2_w.partition_broadcast(P))
+        shift_bc = const.tile([P, D], BF16)
+        nc.scalar.dma_start(out=shift_bc[:], in_=ln2_b.partition_broadcast(P))
+
+        u_sb, a_sb, x_sb = [], [], []
+        for g in range(GROUPS):
+            u_g = inputs.tile([P, GROUP_TILES * D], BF16, name="u%d" % g)
+            a_g = inputs.tile([P, GROUP_TILES * D], BF16, name="a%d" % g)
+            x_g = inputs.tile([P, GROUP_TILES * D], BF16, name="x%d" % g)
+            nc.sync.dma_start(out=u_g[:], in_=group_rows(u, g))
+            nc.sync.dma_start(out=a_g[:], in_=group_rows(attn_out, g))
+            nc.sync.dma_start(out=x_g[:], in_=group_rows(src_norm, g))
+            u_sb.append(u_g)
+            a_sb.append(a_g)
+            x_sb.append(x_g)
+
+        ident = const.tile([P, P], F32)
+        make_identity(nc, ident[:])
+        eps_col = const.tile([P, 1], F32)
+        nc.vector.memset(eps_col[:], EPS)
+
+        w_grouped = const.tile([P, PASSES, D * 4], BF16, align_bytes=64)
+        w_codes = const.tile([P, PASSES, D], U32, align_bytes=64)
+        w_scales = const.tile([P, PASSES, D], U8, align_bytes=64)
+        for c in range(PASSES):
+            rows_of_pass = w_raw[:, c * HALVES : (c + 1) * HALVES, :].rearrange("p h (e n) -> p n (h e)", e=2)
+            words_of_pass = w_grouped[:, c, :].rearrange("p (n t) -> p n t", t=4)
+            if c == 0:
+                nc.vector.tensor_copy(out=words_of_pass, in_=rows_of_pass)
+            else:
+                nc.scalar.copy(out=words_of_pass, in_=rows_of_pass)
+        for c in range(PASSES):
+            nc.vector.quantize_mx(
+                out=w_codes[:, c, :].bitcast(FP8X4), scales=w_scales[:, c, :], in_=w_grouped[:, c, :]
+            )
+
+        for g in range(GROUPS):
+            res = per_group.tile([P, GROUP_TILES * D], BF16)
+            nc.vector.tensor_tensor(out=res[:], in0=u_sb[g][:], in1=a_sb[g][:], op=ALU.add)
+            x_plus_shift = per_group.tile([P, GROUP_TILES, D], F32)
+            nc.vector.tensor_tensor(
+                out=x_plus_shift[:],
+                in0=x_sb[g][:].rearrange("p (n d) -> p n d", n=GROUP_TILES),
+                in1=shift_bc[:].unsqueeze(1).to_broadcast([P, GROUP_TILES, D]),
+                op=ALU.add,
+            )
+            result = per_group.tile([P, GROUP_TILES, D], F32)
+            cat_words = [res[:].bitcast(F32), x_sb[g][:].bitcast(F32)]
+
+            for pair in range(GROUP_TILES // PAIR):
+                grouped = per_pair.tile([P, PAIR * PASSES * P * 4], BF16, align_bytes=64)
+                grouped_words = grouped[:].bitcast(F32).rearrange(
+                    "p (i c r h) -> p i c r h", i=PAIR, c=PASSES, h=HALVES
+                )
+                for i in range(PAIR):
+                    n = pair * PAIR + i
+                    cat_t = psum_t.tile([P, PASSES * HALVES, P], F32)
+                    for c in range(PASSES):
+                        for h in range(HALVES):
+                            first = n * (D // 2) + h * P
+                            nc.tensor.transpose(
+                                cat_t[:, c * HALVES + h, :], cat_words[c][:, first : first + P], ident[:]
+                            )
+                    nc.scalar.copy(
+                        out=grouped_words[:, i], in_=cat_t[:].rearrange("p (c h) r -> p c r h", h=HALVES)
+                    )
+                codes = per_pair.tile([P, PAIR * PASSES * P], U32, align_bytes=64)
+                scales = per_pair.tile([P, PAIR * PASSES * P], U8, align_bytes=64)
+                nc.vector.quantize_mx(out=codes[:].bitcast(FP8X4), scales=scales[:], in_=grouped[:])
+
+                row_sum = per_pair.tile([P, PAIR], F32)
+                neg_mean = per_pair.tile([P, PAIR], F32)
+                sq_sum = per_pair.tile([P, PAIR], F32)
+                std = per_pair.tile([P, PAIR], F32)
+                rstd = per_pair.tile([P, PAIR], F32)
+                zb = []
+                for i in range(PAIR):
+                    z = psum_z.tile([P, D], F32)
+                    for c in range(PASSES):
+                        cols = slice((i * PASSES + c) * P, (i * PASSES + c + 1) * P)
+                        nc.tensor.matmul_mx(
+                            out=z[:],
+                            lhsT=codes[:, cols].bitcast(FP8X4),
+                            lhsT_scale=scales[:, cols],
+                            rhs=w_codes[:, c, :].bitcast(FP8X4),
+                            rhs_scale=w_scales[:, c, :],
+                            start=(c == 0),
+                            stop=(c == PASSES - 1),
+                        )
+                    zb_i = per_tile.tile([P, D], F32, name="zb")
+                    nc.vector.scalar_tensor_tensor(
+                        out=zb_i[:], in0=z[:], scalar=1.0, in1=b_bc[:], op0=ALU.mult, op1=ALU.add,
+                        accum_out=row_sum[:, i : i + 1],
+                    )
+                    zb.append(zb_i)
+                nc.scalar.mul(out=neg_mean[:], in_=row_sum[:], mul=-1.0 / D)
+                for i in range(PAIR):
+                    squares = per_tile.tile([P, D], BF16)
+                    nc.scalar.activation(
+                        out=squares[:], in_=zb[i][:], func=ACT.Square, bias=neg_mean[:, i : i + 1], scale=1.0,
+                        accum_out=sq_sum[:, i : i + 1],
+                    )
+                nc.scalar.activation(out=std[:], in_=sq_sum[:], func=ACT.Sqrt, bias=eps_col[:], scale=1.0 / D)
+                nc.vector.reciprocal(out=rstd[:], in_=std[:])
+                for i in range(PAIR):
+                    n = pair * PAIR + i
+                    gained = per_tile.tile([P, D], F32)
+                    nc.vector.scalar_tensor_tensor(
+                        out=gained[:], in0=zb[i][:], scalar=neg_mean[:, i : i + 1], in1=gain_bc[:],
+                        op0=ALU.add, op1=ALU.mult,
+                    )
+                    nc.vector.scalar_tensor_tensor(
+                        out=result[:, n, :], in0=gained[:], scalar=rstd[:, i : i + 1], in1=x_plus_shift[:, n, :],
+                        op0=ALU.mult, op1=ALU.add,
+                    )
+            nc.sync.dma_start(out=group_rows(out, g), in_=result[:].rearrange("p n d -> p (n d)"))

@@ -14,12 +14,12 @@ ACT = mybir.ActivationFunctionType
 P = 128
 ROWS = 512 * 8
 D = 512
+BLOCKS = D // P
 PASSES = 2
 HALVES = 2
-GROUP_TILES = 4
-GROUP_ROWS = GROUP_TILES * P
-GROUPS = ROWS // GROUP_ROWS
 PAIR = 2
+PAIR_ROWS = PAIR * P
+PAIRS = ROWS // PAIR_ROWS
 EPS = 1e-5
 
 FLOPS = 2 * ROWS * (PASSES * 512) * D
@@ -28,19 +28,22 @@ FLOPS = 2 * ROWS * (PASSES * 512) * D
 def tile_stulayer_pb_t_kernel(tc, u, attn_out, src_norm, w_out, b_out, ln2_w, ln2_b, out):
     nc = tc.nc
 
-    def group_rows(x, g):
-        rows = x.flatten_outer_dims()[g * GROUP_ROWS : (g + 1) * GROUP_ROWS, :]
-        return rows.rearrange("(p n) d -> p (n d)", n=GROUP_TILES)
+    def pair_rows(x, j):
+        rows = x.flatten_outer_dims()[j * PAIR_ROWS : (j + 1) * PAIR_ROWS, :]
+        return rows.rearrange("(p i) d -> p (i d)", i=PAIR)
 
     with ExitStack() as pools:
         const = pools.enter_context(tc.tile_pool(name="const", bufs=1))
         inputs = pools.enter_context(tc.tile_pool(name="inputs", bufs=1))
-        per_group = pools.enter_context(tc.tile_pool(name="per_group", bufs=2))
-        per_pair = pools.enter_context(tc.tile_pool(name="per_pair", bufs=3))
-        per_tile = pools.enter_context(tc.tile_pool(name="per_tile", bufs=4))
-        psum_t = pools.enter_context(tc.psum_pool(name="psum_t", bufs=4))
-        psum_z = pools.enter_context(tc.psum_pool(name="psum_z", bufs=4))
+        two = pools.enter_context(tc.tile_pool(name="two", bufs=2))
+        three = pools.enter_context(tc.tile_pool(name="three", bufs=3))
+        six = pools.enter_context(tc.tile_pool(name="six", bufs=6))
+        psum = pools.enter_context(tc.psum_pool(name="psum", bufs=PAIR))
 
+        vec_rows = const.tile([P, P], BF16)
+        nc.vector.memset(vec_rows[:], 0.0)
+        nc.scalar.dma_start(out=vec_rows[0:BLOCKS, :], in_=ln2_w.rearrange("(f p) -> f p", p=P))
+        nc.scalar.dma_start(out=vec_rows[BLOCKS : 2 * BLOCKS, :], in_=ln2_b.rearrange("(f p) -> f p", p=P))
         w_raw = const.tile([P, PASSES * HALVES, 2 * D], BF16)
         nc.scalar.dma_start(
             out=w_raw[:],
@@ -48,22 +51,18 @@ def tile_stulayer_pb_t_kernel(tc, u, attn_out, src_norm, w_out, b_out, ln2_w, ln
         )
         b_bc = const.tile([P, D], BF16)
         nc.scalar.dma_start(out=b_bc[:], in_=b_out.partition_broadcast(P))
-        gain_bc = const.tile([P, D], BF16)
-        nc.scalar.dma_start(out=gain_bc[:], in_=ln2_w.partition_broadcast(P))
-        shift_bc = const.tile([P, D], BF16)
-        nc.scalar.dma_start(out=shift_bc[:], in_=ln2_b.partition_broadcast(P))
 
         u_sb, a_sb, x_sb = [], [], []
-        for g in range(GROUPS):
-            u_g = inputs.tile([P, GROUP_TILES * D], BF16, name="u%d" % g)
-            a_g = inputs.tile([P, GROUP_TILES * D], BF16, name="a%d" % g)
-            x_g = inputs.tile([P, GROUP_TILES * D], BF16, name="x%d" % g)
-            nc.sync.dma_start(out=u_g[:], in_=group_rows(u, g))
-            nc.sync.dma_start(out=a_g[:], in_=group_rows(attn_out, g))
-            nc.sync.dma_start(out=x_g[:], in_=group_rows(src_norm, g))
-            u_sb.append(u_g)
-            a_sb.append(a_g)
-            x_sb.append(x_g)
+        for j in range(PAIRS):
+            u_j = inputs.tile([P, PAIR * D], BF16, name="u%d" % j)
+            a_j = inputs.tile([P, PAIR * D], BF16, name="a%d" % j)
+            x_j = inputs.tile([P, PAIR * D], BF16, name="x%d" % j)
+            nc.sync.dma_start(out=u_j[:], in_=pair_rows(u, j))
+            nc.sync.dma_start(out=a_j[:], in_=pair_rows(attn_out, j))
+            nc.sync.dma_start(out=x_j[:], in_=pair_rows(src_norm, j))
+            u_sb.append(u_j)
+            a_sb.append(a_j)
+            x_sb.append(x_j)
 
         ident = const.tile([P, P], F32)
         make_identity(nc, ident[:])
@@ -73,95 +72,143 @@ def tile_stulayer_pb_t_kernel(tc, u, attn_out, src_norm, w_out, b_out, ln2_w, ln
         w_grouped = const.tile([P, PASSES, D * 4], BF16, align_bytes=64)
         w_codes = const.tile([P, PASSES, D], U32, align_bytes=64)
         w_scales = const.tile([P, PASSES, D], U8, align_bytes=64)
-        for c in range(PASSES):
-            rows_of_pass = w_raw[:, c * HALVES : (c + 1) * HALVES, :].rearrange("p h (e n) -> p n (h e)", e=2)
-            words_of_pass = w_grouped[:, c, :].rearrange("p (n t) -> p n t", t=4)
-            if c == 0:
-                nc.vector.tensor_copy(out=words_of_pass, in_=rows_of_pass)
-            else:
-                nc.scalar.copy(out=words_of_pass, in_=rows_of_pass)
-        for c in range(PASSES):
-            nc.vector.quantize_mx(
-                out=w_codes[:, c, :].bitcast(FP8X4), scales=w_scales[:, c, :], in_=w_grouped[:, c, :]
-            )
+        vec_rows_f32 = const.tile([P, P], F32)
+        vec_cols = const.tile([P, 2 * BLOCKS], F32)
 
-        for g in range(GROUPS):
-            res = per_group.tile([P, GROUP_TILES * D], BF16)
-            nc.vector.tensor_tensor(out=res[:], in0=u_sb[g][:], in1=a_sb[g][:], op=ALU.add)
-            x_plus_shift = per_group.tile([P, GROUP_TILES, D], F32)
-            nc.vector.tensor_tensor(
-                out=x_plus_shift[:],
-                in0=x_sb[g][:].rearrange("p (n d) -> p n d", n=GROUP_TILES),
-                in1=shift_bc[:].unsqueeze(1).to_broadcast([P, GROUP_TILES, D]),
-                op=ALU.add,
-            )
-            result = per_group.tile([P, GROUP_TILES, D], F32)
-            cat_words = [res[:].bitcast(F32), x_sb[g][:].bitcast(F32)]
+        def prepare_gain_shift():
+            nc.vector.tensor_copy(out=vec_rows_f32[:], in_=vec_rows[:])
+            vec_t = psum.tile([P, PASSES * HALVES, P], F32, tag="cat_t")
+            nc.tensor.transpose(vec_t[:, 0, :], vec_rows_f32[:], ident[:])
+            nc.vector.tensor_copy(out=vec_cols[:], in_=vec_t[:, 0, 0 : 2 * BLOCKS])
 
-            for pair in range(GROUP_TILES // PAIR):
-                grouped = per_pair.tile([P, PAIR * PASSES * P * 4], BF16, align_bytes=64)
-                grouped_words = grouped[:].bitcast(F32).rearrange(
-                    "p (i c r h) -> p i c r h", i=PAIR, c=PASSES, h=HALVES
+        def prepare_weight():
+            for c in range(PASSES):
+                rows_of_pass = w_raw[:, c * HALVES : (c + 1) * HALVES, :].rearrange("p h (e n) -> p n (h e)", e=2)
+                words_of_pass = w_grouped[:, c, :].rearrange("p (n t) -> p n t", t=4)
+                if c == 0:
+                    nc.vector.tensor_copy(out=words_of_pass, in_=rows_of_pass)
+                else:
+                    nc.scalar.copy(out=words_of_pass, in_=rows_of_pass)
+            for c in range(PASSES):
+                nc.vector.quantize_mx(
+                    out=w_codes[:, c, :].bitcast(FP8X4), scales=w_scales[:, c, :], in_=w_grouped[:, c, :]
                 )
-                for i in range(PAIR):
-                    n = pair * PAIR + i
-                    cat_t = psum_t.tile([P, PASSES * HALVES, P], F32)
-                    for c in range(PASSES):
-                        for h in range(HALVES):
-                            first = n * (D // 2) + h * P
-                            nc.tensor.transpose(
-                                cat_t[:, c * HALVES + h, :], cat_words[c][:, first : first + P], ident[:]
-                            )
-                    nc.scalar.copy(
-                        out=grouped_words[:, i], in_=cat_t[:].rearrange("p (c h) r -> p c r h", h=HALVES)
-                    )
-                codes = per_pair.tile([P, PAIR * PASSES * P], U32, align_bytes=64)
-                scales = per_pair.tile([P, PAIR * PASSES * P], U8, align_bytes=64)
-                nc.vector.quantize_mx(out=codes[:].bitcast(FP8X4), scales=scales[:], in_=grouped[:])
 
-                row_sum = per_pair.tile([P, PAIR], F32)
-                neg_mean = per_pair.tile([P, PAIR], F32)
-                sq_sum = per_pair.tile([P, PAIR], F32)
-                std = per_pair.tile([P, PAIR], F32)
-                rstd = per_pair.tile([P, PAIR], F32)
-                zb = []
-                for i in range(PAIR):
-                    z = psum_z.tile([P, D], F32)
-                    for c in range(PASSES):
-                        cols = slice((i * PASSES + c) * P, (i * PASSES + c + 1) * P)
-                        nc.tensor.matmul_mx(
-                            out=z[:],
-                            lhsT=codes[:, cols].bitcast(FP8X4),
-                            lhsT_scale=scales[:, cols],
-                            rhs=w_codes[:, c, :].bitcast(FP8X4),
-                            rhs_scale=w_scales[:, c, :],
-                            start=(c == 0),
-                            stop=(c == PASSES - 1),
-                        )
-                    zb_i = per_tile.tile([P, D], F32, name="zb")
-                    nc.vector.scalar_tensor_tensor(
-                        out=zb_i[:], in0=z[:], scalar=1.0, in1=b_bc[:], op0=ALU.mult, op1=ALU.add,
-                        accum_out=row_sum[:, i : i + 1],
+        res, grouped, codes, scales, zb, y, w_t, result = {}, {}, {}, {}, {}, {}, {}, {}
+        row_sum, neg_mean, sq_sum, std, rstd = {}, {}, {}, {}, {}
+
+        def add_inputs(j):
+            res[j] = three.tile([P, PAIR * D], BF16, name="res")
+            nc.vector.tensor_tensor(out=res[j][:], in0=u_sb[j][:], in1=a_sb[j][:], op=ALU.add)
+
+        def transpose_in(j):
+            grouped[j] = three.tile([P, PAIR * PASSES * P * 4], BF16, align_bytes=64, name="grouped")
+            grouped_words = grouped[j][:].bitcast(F32).rearrange(
+                "p (i c r h) -> p i c r h", i=PAIR, c=PASSES, h=HALVES
+            )
+            cat_words = [res[j][:].bitcast(F32), x_sb[j][:].bitcast(F32)]
+            for i in range(PAIR):
+                cat_t = psum.tile([P, PASSES * HALVES, P], F32, tag="cat_t")
+                for c in range(PASSES):
+                    for h in range(HALVES):
+                        first = i * (D // 2) + h * P
+                        nc.tensor.transpose(cat_t[:, c * HALVES + h, :], cat_words[c][:, first : first + P], ident[:])
+                nc.scalar.copy(out=grouped_words[:, i], in_=cat_t[:].rearrange("p (c h) r -> p c r h", h=HALVES))
+
+        def quantise(j):
+            codes[j] = two.tile([P, PAIR * PASSES * P], U32, align_bytes=64, name="codes")
+            scales[j] = two.tile([P, PAIR * PASSES * P], U8, align_bytes=64, name="scales")
+            nc.vector.quantize_mx(out=codes[j][:].bitcast(FP8X4), scales=scales[j][:], in_=grouped[j][:])
+
+        def project(j):
+            row_sum[j] = three.tile([P, PAIR], F32, name="row_sum")
+            zb[j] = []
+            for i in range(PAIR):
+                z = psum.tile([P, D], F32, tag="z")
+                for c in range(PASSES):
+                    cols = slice((i * PASSES + c) * P, (i * PASSES + c + 1) * P)
+                    nc.tensor.matmul_mx(
+                        out=z[:],
+                        lhsT=codes[j][:, cols].bitcast(FP8X4),
+                        lhsT_scale=scales[j][:, cols],
+                        rhs=w_codes[:, c, :].bitcast(FP8X4),
+                        rhs_scale=w_scales[:, c, :],
+                        start=(c == 0),
+                        stop=(c == PASSES - 1),
                     )
-                    zb.append(zb_i)
-                nc.scalar.mul(out=neg_mean[:], in_=row_sum[:], mul=-1.0 / D)
-                for i in range(PAIR):
-                    squares = per_tile.tile([P, D], BF16)
+                zb_i = six.tile([P, D], F32, name="zb")
+                nc.vector.scalar_tensor_tensor(
+                    out=zb_i[:], in0=z[:], scalar=1.0, in1=b_bc[:], op0=ALU.mult, op1=ALU.add,
+                    accum_out=row_sum[j][:, i : i + 1],
+                )
+                zb[j].append(zb_i)
+
+        def variance(j):
+            neg_mean[j] = three.tile([P, PAIR], F32, name="neg_mean")
+            sq_sum[j] = three.tile([P, PAIR], F32, name="sq_sum")
+            std[j] = three.tile([P, PAIR], F32, name="std")
+            nc.scalar.mul(out=neg_mean[j][:], in_=row_sum[j][:], mul=-1.0 / D)
+            for i in range(PAIR):
+                squares = two.tile([P, D], BF16, name="squares")
+                nc.scalar.activation(
+                    out=squares[:], in_=zb[j][i][:], func=ACT.Square, bias=neg_mean[j][:, i : i + 1], scale=1.0,
+                    accum_out=sq_sum[j][:, i : i + 1],
+                )
+            nc.scalar.activation(out=std[j][:], in_=sq_sum[j][:], func=ACT.Sqrt, bias=eps_col[:], scale=1.0 / D)
+
+        def normalise(j):
+            rstd[j] = three.tile([P, PAIR], F32, name="rstd")
+            nc.vector.reciprocal(out=rstd[j][:], in_=std[j][:])
+            y[j] = []
+            for i in range(PAIR):
+                y_i = six.tile([P, D], F32, name="y")
+                nc.gpsimd.tensor_scalar(
+                    out=y_i[:], in0=zb[j][i][:], scalar1=neg_mean[j][:, i : i + 1], scalar2=rstd[j][:, i : i + 1],
+                    op0=ALU.add, op1=ALU.mult,
+                )
+                y[j].append(y_i)
+
+        def gain_shift(j):
+            w_t[j] = three.tile([P, BLOCKS, PAIR, P], F32, name="w_t")
+            for bank in range(PAIR):
+                y_t = psum.tile([P, BLOCKS // PAIR, PAIR, P], F32, tag="y_t")
+                for s in range(BLOCKS // PAIR):
+                    f = bank * (BLOCKS // PAIR) + s
+                    for i in range(PAIR):
+                        nc.tensor.transpose(y_t[:, s, i, :], y[j][i][:, f * P : (f + 1) * P], ident[:])
+                for s in range(BLOCKS // PAIR):
+                    f = bank * (BLOCKS // PAIR) + s
                     nc.scalar.activation(
-                        out=squares[:], in_=zb[i][:], func=ACT.Square, bias=neg_mean[:, i : i + 1], scale=1.0,
-                        accum_out=sq_sum[:, i : i + 1],
+                        out=w_t[j][:, f, :, :], in_=y_t[:, s, :, :], func=ACT.Identity,
+                        scale=vec_cols[:, f : f + 1], bias=vec_cols[:, BLOCKS + f : BLOCKS + f + 1],
                     )
-                nc.scalar.activation(out=std[:], in_=sq_sum[:], func=ACT.Sqrt, bias=eps_col[:], scale=1.0 / D)
-                nc.vector.reciprocal(out=rstd[:], in_=std[:])
-                for i in range(PAIR):
-                    n = pair * PAIR + i
-                    gained = per_tile.tile([P, D], F32)
-                    nc.vector.scalar_tensor_tensor(
-                        out=gained[:], in0=zb[i][:], scalar=neg_mean[:, i : i + 1], in1=gain_bc[:],
-                        op0=ALU.add, op1=ALU.mult,
-                    )
-                    nc.vector.scalar_tensor_tensor(
-                        out=result[:, n, :], in0=gained[:], scalar=rstd[:, i : i + 1], in1=x_plus_shift[:, n, :],
-                        op0=ALU.mult, op1=ALU.add,
-                    )
-            nc.sync.dma_start(out=group_rows(out, g), in_=result[:].rearrange("p n d -> p (n d)"))
+
+        def finish(j):
+            result[j] = three.tile([P, PAIR * D], F32, name="result")
+            for i in range(PAIR):
+                w_ps = psum.tile([P, D], F32, tag="w_ps")
+                for f in range(BLOCKS):
+                    nc.tensor.transpose(w_ps[:, f * P : (f + 1) * P], w_t[j][:, f, i, :], ident[:])
+                cols = slice(i * D, (i + 1) * D)
+                nc.vector.tensor_tensor(out=result[j][:, cols], in0=w_ps[:], in1=x_sb[j][:, cols], op=ALU.add)
+            nc.sync.dma_start(out=pair_rows(out, j), in_=result[j][:])
+
+        def run(stage, j):
+            if 0 <= j < PAIRS:
+                stage(j)
+
+        with tc.manual_schedule():
+            prepare_gain_shift()
+            add_inputs(0)
+            add_inputs(1)
+            transpose_in(0)
+            prepare_weight()
+            for k in range(1, PAIRS + 4):
+                run(quantise, k - 1)
+                run(variance, k - 2)
+                run(finish, k - 4)
+                run(normalise, k - 2)
+                run(gain_shift, k - 3)
+                run(add_inputs, k + 1)
+                run(transpose_in, k)
+                run(project, k - 1)

@@ -17,6 +17,7 @@ D = 512
 BLOCKS = D // P
 PASSES = 2
 HALVES = 2
+TILES = ROWS // P
 PAIR = 2
 PAIR_ROWS = PAIR * P
 PAIRS = ROWS // PAIR_ROWS
@@ -37,8 +38,9 @@ def tile_stulayer_pb_t_kernel(tc, u, attn_out, src_norm, w_out, b_out, ln2_w, ln
         inputs = pools.enter_context(tc.tile_pool(name="inputs", bufs=1))
         two = pools.enter_context(tc.tile_pool(name="two", bufs=2))
         three = pools.enter_context(tc.tile_pool(name="three", bufs=3))
+        four = pools.enter_context(tc.tile_pool(name="four", bufs=4))
         six = pools.enter_context(tc.tile_pool(name="six", bufs=6))
-        psum = pools.enter_context(tc.psum_pool(name="psum", bufs=PAIR))
+        psum = pools.enter_context(tc.psum_pool(name="psum", bufs=2))
 
         vec_rows = const.tile([P, P], BF16)
         nc.vector.memset(vec_rows[:], 0.0)
@@ -66,8 +68,8 @@ def tile_stulayer_pb_t_kernel(tc, u, attn_out, src_norm, w_out, b_out, ln2_w, ln
 
         ident = const.tile([P, P], F32)
         make_identity(nc, ident[:])
-        eps_col = const.tile([P, 1], F32)
-        nc.vector.memset(eps_col[:], EPS)
+        minus_half = const.tile([P, 1], F32)
+        nc.vector.memset(minus_half[:], -0.5)
 
         w_grouped = const.tile([P, PASSES, D * 4], BF16, align_bytes=64)
         w_codes = const.tile([P, PASSES, D], U32, align_bytes=64)
@@ -94,108 +96,105 @@ def tile_stulayer_pb_t_kernel(tc, u, attn_out, src_norm, w_out, b_out, ln2_w, ln
                     out=w_codes[:, c, :].bitcast(FP8X4), scales=w_scales[:, c, :], in_=w_grouped[:, c, :]
                 )
 
-        res, grouped, codes, scales, zb, y, w_t, result = {}, {}, {}, {}, {}, {}, {}, {}
-        row_sum, neg_mean, sq_sum, std, rstd = {}, {}, {}, {}, {}
+        res, grouped, codes, scales, z, zb, y, w_t, result = {}, {}, {}, {}, {}, {}, {}, {}, {}
+        neg_mean, sq_sum, rstd = {}, {}, {}
 
-        def add_inputs(j):
-            res[j] = three.tile([P, PAIR * D], BF16, name="res")
-            nc.vector.tensor_tensor(out=res[j][:], in0=u_sb[j][:], in1=a_sb[j][:], op=ALU.add)
+        def add_inputs(m):
+            j, i = divmod(m, PAIR)
+            cols = slice(i * D, (i + 1) * D)
+            res[m] = three.tile([P, D], BF16, name="res")
+            nc.vector.tensor_tensor(out=res[m][:], in0=u_sb[j][:, cols], in1=a_sb[j][:, cols], op=ALU.add)
 
-        def transpose_in(j):
-            grouped[j] = three.tile([P, PAIR * PASSES * P * 4], BF16, align_bytes=64, name="grouped")
-            grouped_words = grouped[j][:].bitcast(F32).rearrange(
-                "p (i c r h) -> p i c r h", i=PAIR, c=PASSES, h=HALVES
+        def transpose_in(m):
+            j, i = divmod(m, PAIR)
+            cat_words = [res[m][:].bitcast(F32), x_sb[j][:].bitcast(F32)[:, i * (D // 2) : (i + 1) * (D // 2)]]
+            cat_t = psum.tile([P, PASSES * HALVES, P], F32, tag="cat_t")
+            for c in range(PASSES):
+                for h in range(HALVES):
+                    nc.tensor.transpose(cat_t[:, c * HALVES + h, :], cat_words[c][:, h * P : (h + 1) * P], ident[:])
+            grouped[m] = three.tile([P, PASSES * P * 4], BF16, align_bytes=64, name="grouped")
+            nc.scalar.copy(
+                out=grouped[m][:].bitcast(F32).rearrange("p (c r h) -> p c r h", c=PASSES, h=HALVES),
+                in_=cat_t[:].rearrange("p (c h) r -> p c r h", h=HALVES),
             )
-            cat_words = [res[j][:].bitcast(F32), x_sb[j][:].bitcast(F32)]
-            for i in range(PAIR):
-                cat_t = psum.tile([P, PASSES * HALVES, P], F32, tag="cat_t")
-                for c in range(PASSES):
-                    for h in range(HALVES):
-                        first = i * (D // 2) + h * P
-                        nc.tensor.transpose(cat_t[:, c * HALVES + h, :], cat_words[c][:, first : first + P], ident[:])
-                nc.scalar.copy(out=grouped_words[:, i], in_=cat_t[:].rearrange("p (c h) r -> p c r h", h=HALVES))
 
-        def quantise(j):
-            codes[j] = two.tile([P, PAIR * PASSES * P], U32, align_bytes=64, name="codes")
-            scales[j] = two.tile([P, PAIR * PASSES * P], U8, align_bytes=64, name="scales")
-            nc.vector.quantize_mx(out=codes[j][:].bitcast(FP8X4), scales=scales[j][:], in_=grouped[j][:])
+        def quantise(m):
+            codes[m] = three.tile([P, PASSES * P], U32, align_bytes=64, name="codes")
+            scales[m] = three.tile([P, PASSES * P], U8, align_bytes=64, name="scales")
+            nc.vector.quantize_mx(out=codes[m][:].bitcast(FP8X4), scales=scales[m][:], in_=grouped[m][:])
 
-        def project(j):
-            row_sum[j] = three.tile([P, PAIR], F32, name="row_sum")
-            zb[j] = []
-            for i in range(PAIR):
-                z = psum.tile([P, D], F32, tag="z")
-                for c in range(PASSES):
-                    cols = slice((i * PASSES + c) * P, (i * PASSES + c + 1) * P)
-                    nc.tensor.matmul_mx(
-                        out=z[:],
-                        lhsT=codes[j][:, cols].bitcast(FP8X4),
-                        lhsT_scale=scales[j][:, cols],
-                        rhs=w_codes[:, c, :].bitcast(FP8X4),
-                        rhs_scale=w_scales[:, c, :],
-                        start=(c == 0),
-                        stop=(c == PASSES - 1),
-                    )
-                zb_i = six.tile([P, D], F32, name="zb")
-                nc.vector.scalar_tensor_tensor(
-                    out=zb_i[:], in0=z[:], scalar=1.0, in1=b_bc[:], op0=ALU.mult, op1=ALU.add,
-                    accum_out=row_sum[j][:, i : i + 1],
+        def project(m):
+            z[m] = psum.tile([P, D], F32, tag="z", name="z")
+            for c in range(PASSES):
+                cols = slice(c * P, (c + 1) * P)
+                nc.tensor.matmul_mx(
+                    out=z[m][:],
+                    lhsT=codes[m][:, cols].bitcast(FP8X4),
+                    lhsT_scale=scales[m][:, cols],
+                    rhs=w_codes[:, c, :].bitcast(FP8X4),
+                    rhs_scale=w_scales[:, c, :],
+                    start=(c == 0),
+                    stop=(c == PASSES - 1),
                 )
-                zb[j].append(zb_i)
 
-        def variance(j):
-            neg_mean[j] = three.tile([P, PAIR], F32, name="neg_mean")
-            sq_sum[j] = three.tile([P, PAIR], F32, name="sq_sum")
-            std[j] = three.tile([P, PAIR], F32, name="std")
-            nc.scalar.mul(out=neg_mean[j][:], in_=row_sum[j][:], mul=-1.0 / D)
-            for i in range(PAIR):
-                squares = two.tile([P, D], BF16, name="squares")
+        def add_bias(m):
+            zb[m] = four.tile([P, D], F32, name="zb")
+            row_sum = four.tile([P, 1], F32, name="row_sum")
+            nc.vector.scalar_tensor_tensor(
+                out=zb[m][:], in0=z[m][:], scalar=1.0, in1=b_bc[:], op0=ALU.mult, op1=ALU.add, accum_out=row_sum[:]
+            )
+            neg_mean[m] = four.tile([P, 1], F32, name="neg_mean")
+            nc.vector.tensor_scalar_mul(out=neg_mean[m][:], in0=row_sum[:], scalar1=-1.0 / D)
+
+        def square_sum(m):
+            squares = two.tile([P, D], BF16, name="squares")
+            sq_sum[m] = four.tile([P, 1], F32, name="sq_sum")
+            nc.scalar.activation(
+                out=squares[:], in_=zb[m][:], func=ACT.Square, bias=neg_mean[m][:], scale=1.0, accum_out=sq_sum[m][:]
+            )
+
+        def normalise(m):
+            var_eps = four.tile([P, 1], F32, name="var_eps")
+            nc.gpsimd.tensor_scalar(
+                out=var_eps[:], in0=sq_sum[m][:], scalar1=1.0 / D, scalar2=EPS, op0=ALU.mult, op1=ALU.add
+            )
+            rstd[m] = four.tile([P, 1], F32, name="rstd")
+            nc.gpsimd.tensor_tensor(out=rstd[m][:], in0=var_eps[:], in1=minus_half[:], op=ALU.pow)
+            y[m] = six.tile([P, D], F32, name="y")
+            nc.gpsimd.tensor_scalar(
+                out=y[m][:], in0=zb[m][:], scalar1=neg_mean[m][:], scalar2=rstd[m][:], op0=ALU.add, op1=ALU.mult
+            )
+
+        def gain_shift(s):
+            j, bank = divmod(s, PAIR)
+            if bank == 0:
+                w_t[j] = three.tile([P, BLOCKS, PAIR, P], F32, name="w_t")
+            blocks = range(bank * (BLOCKS // PAIR), (bank + 1) * (BLOCKS // PAIR))
+            y_t = psum.tile([P, BLOCKS // PAIR, PAIR, P], F32, tag="y_t")
+            for slot, f in enumerate(blocks):
+                for i in range(PAIR):
+                    nc.tensor.transpose(y_t[:, slot, i, :], y[j * PAIR + i][:, f * P : (f + 1) * P], ident[:])
+            for slot, f in enumerate(blocks):
                 nc.scalar.activation(
-                    out=squares[:], in_=zb[j][i][:], func=ACT.Square, bias=neg_mean[j][:, i : i + 1], scale=1.0,
-                    accum_out=sq_sum[j][:, i : i + 1],
+                    out=w_t[j][:, f, :, :], in_=y_t[:, slot, :, :], func=ACT.Identity,
+                    scale=vec_cols[:, f : f + 1], bias=vec_cols[:, BLOCKS + f : BLOCKS + f + 1],
                 )
-            nc.scalar.activation(out=std[j][:], in_=sq_sum[j][:], func=ACT.Sqrt, bias=eps_col[:], scale=1.0 / D)
 
-        def normalise(j):
-            rstd[j] = three.tile([P, PAIR], F32, name="rstd")
-            nc.vector.reciprocal(out=rstd[j][:], in_=std[j][:])
-            y[j] = []
-            for i in range(PAIR):
-                y_i = six.tile([P, D], F32, name="y")
-                nc.gpsimd.tensor_scalar(
-                    out=y_i[:], in0=zb[j][i][:], scalar1=neg_mean[j][:, i : i + 1], scalar2=rstd[j][:, i : i + 1],
-                    op0=ALU.add, op1=ALU.mult,
-                )
-                y[j].append(y_i)
+        def finish(m):
+            j, i = divmod(m, PAIR)
+            if i == 0:
+                result[j] = three.tile([P, PAIR * D], F32, name="result")
+            w_ps = psum.tile([P, D], F32, tag="w_ps")
+            for f in range(BLOCKS):
+                nc.tensor.transpose(w_ps[:, f * P : (f + 1) * P], w_t[j][:, f, i, :], ident[:])
+            cols = slice(i * D, (i + 1) * D)
+            nc.vector.tensor_tensor(out=result[j][:, cols], in0=w_ps[:], in1=x_sb[j][:, cols], op=ALU.add)
+            if i == PAIR - 1:
+                nc.sync.dma_start(out=pair_rows(out, j), in_=result[j][:])
 
-        def gain_shift(j):
-            w_t[j] = three.tile([P, BLOCKS, PAIR, P], F32, name="w_t")
-            for bank in range(PAIR):
-                y_t = psum.tile([P, BLOCKS // PAIR, PAIR, P], F32, tag="y_t")
-                for s in range(BLOCKS // PAIR):
-                    f = bank * (BLOCKS // PAIR) + s
-                    for i in range(PAIR):
-                        nc.tensor.transpose(y_t[:, s, i, :], y[j][i][:, f * P : (f + 1) * P], ident[:])
-                for s in range(BLOCKS // PAIR):
-                    f = bank * (BLOCKS // PAIR) + s
-                    nc.scalar.activation(
-                        out=w_t[j][:, f, :, :], in_=y_t[:, s, :, :], func=ACT.Identity,
-                        scale=vec_cols[:, f : f + 1], bias=vec_cols[:, BLOCKS + f : BLOCKS + f + 1],
-                    )
-
-        def finish(j):
-            result[j] = three.tile([P, PAIR * D], F32, name="result")
-            for i in range(PAIR):
-                w_ps = psum.tile([P, D], F32, tag="w_ps")
-                for f in range(BLOCKS):
-                    nc.tensor.transpose(w_ps[:, f * P : (f + 1) * P], w_t[j][:, f, i, :], ident[:])
-                cols = slice(i * D, (i + 1) * D)
-                nc.vector.tensor_tensor(out=result[j][:, cols], in0=w_ps[:], in1=x_sb[j][:, cols], op=ALU.add)
-            nc.sync.dma_start(out=pair_rows(out, j), in_=result[j][:])
-
-        def run(stage, j):
-            if 0 <= j < PAIRS:
-                stage(j)
+        def run(stage, m):
+            if 0 <= m < TILES:
+                stage(m)
 
         with tc.manual_schedule():
             prepare_gain_shift()
@@ -203,12 +202,13 @@ def tile_stulayer_pb_t_kernel(tc, u, attn_out, src_norm, w_out, b_out, ln2_w, ln
             add_inputs(1)
             transpose_in(0)
             prepare_weight()
-            for k in range(1, PAIRS + 4):
-                run(quantise, k - 1)
-                run(variance, k - 2)
-                run(finish, k - 4)
-                run(normalise, k - 2)
-                run(gain_shift, k - 3)
-                run(add_inputs, k + 1)
-                run(transpose_in, k)
-                run(project, k - 1)
+            for h in range(1, TILES + 9):
+                run(quantise, h - 1)
+                run(add_bias, h - 2)
+                run(square_sum, h - 3)
+                run(finish, h - 8)
+                run(normalise, h - 3)
+                run(gain_shift, h - 6)
+                run(add_inputs, h + 1)
+                run(transpose_in, h)
+                run(project, h - 1)

@@ -22,6 +22,8 @@ PAIR = 2
 PAIR_ROWS = PAIR * P
 PAIRS = ROWS // PAIR_ROWS
 EPS = 1e-5
+ROUNDS_BEFORE_WEIGHT = 4
+LAST_LAG = 13
 
 FLOPS = 2 * ROWS * (PASSES * 512) * D
 
@@ -42,15 +44,15 @@ def tile_stulayer_pb_t_kernel(tc, u, attn_out, src_norm, w_out, b_out, ln2_w, ln
         six = pools.enter_context(tc.tile_pool(name="six", bufs=6))
         psum = pools.enter_context(tc.psum_pool(name="psum", bufs=2))
 
-        vec_rows = const.tile([P, P], BF16)
-        nc.vector.memset(vec_rows[:], 0.0)
-        nc.scalar.dma_start(out=vec_rows[0:BLOCKS, :], in_=ln2_w.rearrange("(f p) -> f p", p=P))
-        nc.scalar.dma_start(out=vec_rows[BLOCKS : 2 * BLOCKS, :], in_=ln2_b.rearrange("(f p) -> f p", p=P))
         w_raw = const.tile([P, PASSES * HALVES, 2 * D], BF16)
         nc.scalar.dma_start(
             out=w_raw[:],
             in_=w_out.rearrange("(s q e) n -> q s (e n)", s=PASSES * HALVES, e=2),
         )
+        vec_rows = const.tile([P, P], BF16)
+        nc.vector.memset(vec_rows[:], 0.0)
+        nc.scalar.dma_start(out=vec_rows[0:BLOCKS, :], in_=ln2_w.rearrange("(f p) -> f p", p=P))
+        nc.scalar.dma_start(out=vec_rows[BLOCKS : 2 * BLOCKS, :], in_=ln2_b.rearrange("(f p) -> f p", p=P))
         b_bc = const.tile([P, D], BF16)
         nc.scalar.dma_start(out=b_bc[:], in_=b_out.partition_broadcast(P))
 
@@ -68,20 +70,14 @@ def tile_stulayer_pb_t_kernel(tc, u, attn_out, src_norm, w_out, b_out, ln2_w, ln
 
         ident = const.tile([P, P], F32)
         make_identity(nc, ident[:])
-        minus_half = const.tile([P, 1], F32)
-        nc.vector.memset(minus_half[:], -0.5)
+        eps_col = const.tile([P, 1], F32)
+        nc.vector.memset(eps_col[:], EPS)
 
         w_grouped = const.tile([P, PASSES, D * 4], BF16, align_bytes=64)
         w_codes = const.tile([P, PASSES, D], U32, align_bytes=64)
         w_scales = const.tile([P, PASSES, D], U8, align_bytes=64)
         vec_rows_f32 = const.tile([P, P], F32)
         vec_cols = const.tile([P, 2 * BLOCKS], F32)
-
-        def prepare_gain_shift():
-            nc.vector.tensor_copy(out=vec_rows_f32[:], in_=vec_rows[:])
-            vec_t = psum.tile([P, PASSES * HALVES, P], F32, tag="cat_t")
-            nc.tensor.transpose(vec_t[:, 0, :], vec_rows_f32[:], ident[:])
-            nc.vector.tensor_copy(out=vec_cols[:], in_=vec_t[:, 0, 0 : 2 * BLOCKS])
 
         def prepare_weight():
             for c in range(PASSES):
@@ -96,8 +92,14 @@ def tile_stulayer_pb_t_kernel(tc, u, attn_out, src_norm, w_out, b_out, ln2_w, ln
                     out=w_codes[:, c, :].bitcast(FP8X4), scales=w_scales[:, c, :], in_=w_grouped[:, c, :]
                 )
 
-        res, grouped, codes, scales, z, zb, y, w_t, result = {}, {}, {}, {}, {}, {}, {}, {}, {}
-        neg_mean, sq_sum, rstd = {}, {}, {}
+        def prepare_gain_shift():
+            nc.vector.tensor_copy(out=vec_rows_f32[:], in_=vec_rows[:])
+            vec_t = psum.tile([P, D], F32, tag="w_ps")
+            nc.tensor.transpose(vec_t[:, 0:P], vec_rows_f32[:], ident[:])
+            nc.vector.tensor_copy(out=vec_cols[:], in_=vec_t[:, 0 : 2 * BLOCKS])
+
+        res, cat_t, grouped, codes, scales, z, zb, y, y_t, w_t, w_ps, result = {}, {}, {}, {}, {}, {}, {}, {}, {}, {}, {}, {}
+        row_sum, neg_mean, sq_sum, std, rstd = {}, {}, {}, {}, {}
 
         def add_inputs(m):
             j, i = divmod(m, PAIR)
@@ -105,17 +107,21 @@ def tile_stulayer_pb_t_kernel(tc, u, attn_out, src_norm, w_out, b_out, ln2_w, ln
             res[m] = three.tile([P, D], BF16, name="res")
             nc.vector.tensor_tensor(out=res[m][:], in0=u_sb[j][:, cols], in1=a_sb[j][:, cols], op=ALU.add)
 
-        def transpose_in(m):
+        def transpose_cat(m):
             j, i = divmod(m, PAIR)
             cat_words = [res[m][:].bitcast(F32), x_sb[j][:].bitcast(F32)[:, i * (D // 2) : (i + 1) * (D // 2)]]
-            cat_t = psum.tile([P, PASSES * HALVES, P], F32, tag="cat_t")
+            cat_t[m] = psum.tile([P, PASSES * HALVES, P], F32, tag="cat_t", name="cat_t")
             for c in range(PASSES):
                 for h in range(HALVES):
-                    nc.tensor.transpose(cat_t[:, c * HALVES + h, :], cat_words[c][:, h * P : (h + 1) * P], ident[:])
+                    nc.tensor.transpose(
+                        cat_t[m][:, c * HALVES + h, :], cat_words[c][:, h * P : (h + 1) * P], ident[:]
+                    )
+
+        def copy_cat(m):
             grouped[m] = three.tile([P, PASSES * P * 4], BF16, align_bytes=64, name="grouped")
             nc.scalar.copy(
                 out=grouped[m][:].bitcast(F32).rearrange("p (c r h) -> p c r h", c=PASSES, h=HALVES),
-                in_=cat_t[:].rearrange("p (c h) r -> p c r h", h=HALVES),
+                in_=cat_t[m][:].rearrange("p (c h) r -> p c r h", h=HALVES),
             )
 
         def quantise(m):
@@ -139,12 +145,15 @@ def tile_stulayer_pb_t_kernel(tc, u, attn_out, src_norm, w_out, b_out, ln2_w, ln
 
         def add_bias(m):
             zb[m] = four.tile([P, D], F32, name="zb")
-            row_sum = four.tile([P, 1], F32, name="row_sum")
+            row_sum[m] = four.tile([P, 1], F32, name="row_sum")
             nc.vector.scalar_tensor_tensor(
-                out=zb[m][:], in0=z[m][:], scalar=1.0, in1=b_bc[:], op0=ALU.mult, op1=ALU.add, accum_out=row_sum[:]
+                out=zb[m][:], in0=z[m][:], scalar=1.0, in1=b_bc[:], op0=ALU.mult, op1=ALU.add,
+                accum_out=row_sum[m][:],
             )
+
+        def minus_mean(m):
             neg_mean[m] = four.tile([P, 1], F32, name="neg_mean")
-            nc.vector.tensor_scalar_mul(out=neg_mean[m][:], in0=row_sum[:], scalar1=-1.0 / D)
+            nc.vector.tensor_scalar_mul(out=neg_mean[m][:], in0=row_sum[m][:], scalar1=-1.0 / D)
 
         def square_sum(m):
             squares = two.tile([P, D], BF16, name="squares")
@@ -153,42 +162,52 @@ def tile_stulayer_pb_t_kernel(tc, u, attn_out, src_norm, w_out, b_out, ln2_w, ln
                 out=squares[:], in_=zb[m][:], func=ACT.Square, bias=neg_mean[m][:], scale=1.0, accum_out=sq_sum[m][:]
             )
 
-        def normalise(m):
-            var_eps = four.tile([P, 1], F32, name="var_eps")
-            nc.gpsimd.tensor_scalar(
-                out=var_eps[:], in0=sq_sum[m][:], scalar1=1.0 / D, scalar2=EPS, op0=ALU.mult, op1=ALU.add
-            )
+        def standard_deviation(m):
+            std[m] = four.tile([P, 1], F32, name="std")
+            nc.scalar.activation(out=std[m][:], in_=sq_sum[m][:], func=ACT.Sqrt, bias=eps_col[:], scale=1.0 / D)
+
+        def invert_std(m):
             rstd[m] = four.tile([P, 1], F32, name="rstd")
-            nc.gpsimd.tensor_tensor(out=rstd[m][:], in0=var_eps[:], in1=minus_half[:], op=ALU.pow)
+            nc.vector.reciprocal(out=rstd[m][:], in_=std[m][:])
+
+        def normalise(m):
             y[m] = six.tile([P, D], F32, name="y")
             nc.gpsimd.tensor_scalar(
                 out=y[m][:], in0=zb[m][:], scalar1=neg_mean[m][:], scalar2=rstd[m][:], op0=ALU.add, op1=ALU.mult
             )
 
+        def blocks_of(bank):
+            return range(bank * (BLOCKS // PAIR), (bank + 1) * (BLOCKS // PAIR))
+
+        def transpose_y(s):
+            j, bank = divmod(s, PAIR)
+            y_t[s] = psum.tile([P, BLOCKS // PAIR, PAIR, P], F32, tag="y_t", name="y_t")
+            for slot, f in enumerate(blocks_of(bank)):
+                for i in range(PAIR):
+                    nc.tensor.transpose(y_t[s][:, slot, i, :], y[j * PAIR + i][:, f * P : (f + 1) * P], ident[:])
+
         def gain_shift(s):
             j, bank = divmod(s, PAIR)
             if bank == 0:
                 w_t[j] = three.tile([P, BLOCKS, PAIR, P], F32, name="w_t")
-            blocks = range(bank * (BLOCKS // PAIR), (bank + 1) * (BLOCKS // PAIR))
-            y_t = psum.tile([P, BLOCKS // PAIR, PAIR, P], F32, tag="y_t")
-            for slot, f in enumerate(blocks):
-                for i in range(PAIR):
-                    nc.tensor.transpose(y_t[:, slot, i, :], y[j * PAIR + i][:, f * P : (f + 1) * P], ident[:])
-            for slot, f in enumerate(blocks):
+            for slot, f in enumerate(blocks_of(bank)):
                 nc.scalar.activation(
-                    out=w_t[j][:, f, :, :], in_=y_t[:, slot, :, :], func=ACT.Identity,
+                    out=w_t[j][:, f, :, :], in_=y_t[s][:, slot, :, :], func=ACT.Identity,
                     scale=vec_cols[:, f : f + 1], bias=vec_cols[:, BLOCKS + f : BLOCKS + f + 1],
                 )
 
-        def finish(m):
+        def transpose_back(m):
+            j, i = divmod(m, PAIR)
+            w_ps[m] = psum.tile([P, D], F32, tag="w_ps", name="w_ps")
+            for f in range(BLOCKS):
+                nc.tensor.transpose(w_ps[m][:, f * P : (f + 1) * P], w_t[j][:, f, i, :], ident[:])
+
+        def add_src(m):
             j, i = divmod(m, PAIR)
             if i == 0:
                 result[j] = three.tile([P, PAIR * D], F32, name="result")
-            w_ps = psum.tile([P, D], F32, tag="w_ps")
-            for f in range(BLOCKS):
-                nc.tensor.transpose(w_ps[:, f * P : (f + 1) * P], w_t[j][:, f, i, :], ident[:])
             cols = slice(i * D, (i + 1) * D)
-            nc.vector.tensor_tensor(out=result[j][:, cols], in0=w_ps[:], in1=x_sb[j][:, cols], op=ALU.add)
+            nc.vector.tensor_tensor(out=result[j][:, cols], in0=w_ps[m][:], in1=x_sb[j][:, cols], op=ALU.add)
             if i == PAIR - 1:
                 nc.sync.dma_start(out=pair_rows(out, j), in_=result[j][:])
 
@@ -196,19 +215,27 @@ def tile_stulayer_pb_t_kernel(tc, u, attn_out, src_norm, w_out, b_out, ln2_w, ln
             if 0 <= m < TILES:
                 stage(m)
 
+        def one_round(h):
+            run(quantise, h - 3)
+            run(add_inputs, h)
+            run(invert_std, h - 7)
+            run(normalise, h - 7)
+            run(add_bias, h - 5)
+            run(add_src, h - 13)
+            run(minus_mean, h - 5)
+            run(copy_cat, h - 2)
+            run(square_sum, h - 6)
+            run(gain_shift, h - 10)
+            run(standard_deviation, h - 6)
+            run(transpose_back, h - 12)
+            run(transpose_y, h - 9)
+            run(transpose_cat, h - 1)
+            run(project, h - 4)
+
         with tc.manual_schedule():
-            prepare_gain_shift()
-            add_inputs(0)
-            add_inputs(1)
-            transpose_in(0)
+            for h in range(ROUNDS_BEFORE_WEIGHT):
+                one_round(h)
             prepare_weight()
-            for h in range(1, TILES + 9):
-                run(quantise, h - 1)
-                run(add_bias, h - 2)
-                run(square_sum, h - 3)
-                run(finish, h - 8)
-                run(normalise, h - 3)
-                run(gain_shift, h - 6)
-                run(add_inputs, h + 1)
-                run(transpose_in, h)
-                run(project, h - 1)
+            prepare_gain_shift()
+            for h in range(ROUNDS_BEFORE_WEIGHT, TILES + LAST_LAG + 1):
+                one_round(h)

@@ -22,7 +22,7 @@ PAIR = 2
 PAIR_ROWS = PAIR * P
 PAIRS = ROWS // PAIR_ROWS
 EPS = 1e-5
-ROUNDS_BEFORE_WEIGHT = 4
+ROUNDS_BEFORE_QUANTISING_WEIGHT = 2
 LAST_LAG = 13
 
 FLOPS = 2 * ROWS * (PASSES * 512) * D
@@ -35,6 +35,10 @@ def tile_stulayer_pb_t_kernel(tc, u, attn_out, src_norm, w_out, b_out, ln2_w, ln
         rows = x.flatten_outer_dims()[j * PAIR_ROWS : (j + 1) * PAIR_ROWS, :]
         return rows.rearrange("(p i) d -> p (i d)", i=PAIR)
 
+    def tile_rows(x, m):
+        j, i = divmod(m, PAIR)
+        return pair_rows(x, j)[:, i * D : (i + 1) * D]
+
     with ExitStack() as pools:
         const = pools.enter_context(tc.tile_pool(name="const", bufs=1))
         inputs = pools.enter_context(tc.tile_pool(name="inputs", bufs=1))
@@ -44,17 +48,18 @@ def tile_stulayer_pb_t_kernel(tc, u, attn_out, src_norm, w_out, b_out, ln2_w, ln
         six = pools.enter_context(tc.tile_pool(name="six", bufs=6))
         psum = pools.enter_context(tc.psum_pool(name="psum", bufs=2))
 
-        w_raw = const.tile([P, PASSES * HALVES, 2 * D], BF16)
-        nc.scalar.dma_start(
-            out=w_raw[:],
-            in_=w_out.rearrange("(s q e) n -> q s (e n)", s=PASSES * HALVES, e=2),
-        )
         vec_rows = const.tile([P, P], BF16)
         nc.vector.memset(vec_rows[:], 0.0)
         nc.scalar.dma_start(out=vec_rows[0:BLOCKS, :], in_=ln2_w.rearrange("(f p) -> f p", p=P))
         nc.scalar.dma_start(out=vec_rows[BLOCKS : 2 * BLOCKS, :], in_=ln2_b.rearrange("(f p) -> f p", p=P))
-        b_bc = const.tile([P, D], BF16)
-        nc.scalar.dma_start(out=b_bc[:], in_=b_out.partition_broadcast(P))
+        b_row = const.tile([P, D], BF16)
+        nc.vector.memset(b_row[:], 0.0)
+        nc.scalar.dma_start(out=b_row[0:1, :], in_=b_out.rearrange("(o d) -> o d", o=1))
+        w_raw = const.tile([P, PASSES * HALVES, 2 * D], BF16)
+        nc.sync.dma_start(
+            out=w_raw[:],
+            in_=w_out.rearrange("(s q e) n -> q s (e n)", s=PASSES * HALVES, e=2),
+        )
 
         u_sb, a_sb, x_sb = [], [], []
         for j in range(PAIRS):
@@ -70,16 +75,21 @@ def tile_stulayer_pb_t_kernel(tc, u, attn_out, src_norm, w_out, b_out, ln2_w, ln
 
         ident = const.tile([P, P], F32)
         make_identity(nc, ident[:])
+        ones = const.tile([P, P], BF16)
+        nc.vector.memset(ones[:], 1.0)
         eps_col = const.tile([P, 1], F32)
         nc.vector.memset(eps_col[:], EPS)
+        first_sqrt = const.tile([P, 1], F32)
+        nc.scalar.activation(out=first_sqrt[:], in_=eps_col[:], func=ACT.Sqrt)
 
         w_grouped = const.tile([P, PASSES, D * 4], BF16, align_bytes=64)
         w_codes = const.tile([P, PASSES, D], U32, align_bytes=64)
         w_scales = const.tile([P, PASSES, D], U8, align_bytes=64)
         vec_rows_f32 = const.tile([P, P], F32)
         vec_cols = const.tile([P, 2 * BLOCKS], F32)
+        b_bc = const.tile([P, D], F32)
 
-        def prepare_weight():
+        def regroup_weight():
             for c in range(PASSES):
                 rows_of_pass = w_raw[:, c * HALVES : (c + 1) * HALVES, :].rearrange("p h (e n) -> p n (h e)", e=2)
                 words_of_pass = w_grouped[:, c, :].rearrange("p (n t) -> p n t", t=4)
@@ -87,6 +97,8 @@ def tile_stulayer_pb_t_kernel(tc, u, attn_out, src_norm, w_out, b_out, ln2_w, ln
                     nc.vector.tensor_copy(out=words_of_pass, in_=rows_of_pass)
                 else:
                     nc.scalar.copy(out=words_of_pass, in_=rows_of_pass)
+
+        def quantise_weight():
             for c in range(PASSES):
                 nc.vector.quantize_mx(
                     out=w_codes[:, c, :].bitcast(FP8X4), scales=w_scales[:, c, :], in_=w_grouped[:, c, :]
@@ -97,6 +109,11 @@ def tile_stulayer_pb_t_kernel(tc, u, attn_out, src_norm, w_out, b_out, ln2_w, ln
             vec_t = psum.tile([P, D], F32, tag="w_ps")
             nc.tensor.transpose(vec_t[:, 0:P], vec_rows_f32[:], ident[:])
             nc.vector.tensor_copy(out=vec_cols[:], in_=vec_t[:, 0 : 2 * BLOCKS])
+
+        def prepare_bias():
+            b_ps = psum.tile([P, D], F32, tag="y_t")
+            nc.tensor.matmul(out=b_ps[:], lhsT=ones[:], rhs=b_row[:], start=True, stop=True)
+            nc.vector.tensor_copy(out=b_bc[:], in_=b_ps[:])
 
         res, cat_t, grouped, codes, scales, z, zb, y, y_t, w_t, w_ps, result = {}, {}, {}, {}, {}, {}, {}, {}, {}, {}, {}, {}
         row_sum, neg_mean, sq_sum, std, rstd = {}, {}, {}, {}, {}
@@ -153,7 +170,9 @@ def tile_stulayer_pb_t_kernel(tc, u, attn_out, src_norm, w_out, b_out, ln2_w, ln
 
         def minus_mean(m):
             neg_mean[m] = four.tile([P, 1], F32, name="neg_mean")
-            nc.vector.tensor_scalar_mul(out=neg_mean[m][:], in0=row_sum[m][:], scalar1=-1.0 / D)
+            nc.gpsimd.tensor_scalar(
+                out=neg_mean[m][:], in0=row_sum[m][:], scalar1=-1.0 / D, scalar2=0.0, op0=ALU.mult, op1=ALU.add
+            )
 
         def square_sum(m):
             squares = two.tile([P, D], BF16, name="squares")
@@ -204,12 +223,11 @@ def tile_stulayer_pb_t_kernel(tc, u, attn_out, src_norm, w_out, b_out, ln2_w, ln
 
         def add_src(m):
             j, i = divmod(m, PAIR)
-            if i == 0:
-                result[j] = three.tile([P, PAIR * D], F32, name="result")
-            cols = slice(i * D, (i + 1) * D)
-            nc.vector.tensor_tensor(out=result[j][:, cols], in0=w_ps[m][:], in1=x_sb[j][:, cols], op=ALU.add)
-            if i == PAIR - 1:
-                nc.sync.dma_start(out=pair_rows(out, j), in_=result[j][:])
+            result[m] = four.tile([P, D], F32, name="result")
+            nc.vector.tensor_tensor(
+                out=result[m][:], in0=w_ps[m][:], in1=x_sb[j][:, i * D : (i + 1) * D], op=ALU.add
+            )
+            nc.sync.dma_start(out=tile_rows(out, m), in_=result[m][:])
 
         def run(stage, m):
             if 0 <= m < TILES:
@@ -221,8 +239,8 @@ def tile_stulayer_pb_t_kernel(tc, u, attn_out, src_norm, w_out, b_out, ln2_w, ln
             run(invert_std, h - 7)
             run(normalise, h - 7)
             run(add_bias, h - 5)
-            run(add_src, h - 13)
             run(minus_mean, h - 5)
+            run(add_src, h - 13)
             run(copy_cat, h - 2)
             run(square_sum, h - 6)
             run(gain_shift, h - 10)
@@ -233,9 +251,11 @@ def tile_stulayer_pb_t_kernel(tc, u, attn_out, src_norm, w_out, b_out, ln2_w, ln
             run(project, h - 4)
 
         with tc.manual_schedule():
-            for h in range(ROUNDS_BEFORE_WEIGHT):
+            regroup_weight()
+            for h in range(ROUNDS_BEFORE_QUANTISING_WEIGHT):
                 one_round(h)
-            prepare_weight()
+            quantise_weight()
+            prepare_bias()
             prepare_gain_shift()
-            for h in range(ROUNDS_BEFORE_WEIGHT, TILES + LAST_LAG + 1):
+            for h in range(ROUNDS_BEFORE_QUANTISING_WEIGHT, TILES + LAST_LAG + 1):
                 one_round(h)

@@ -234,13 +234,13 @@ def tile_stulayer_pb_t_kernel(tc, u, attn_out, src_norm, w_out, b_out, ln2_w, ln
                 stage(m)
 
         def one_round(h):
+            run(add_bias, h - 5)
+            run(minus_mean, h - 5)
             run(quantise, h - 3)
+            run(add_src, h - 13)
             run(add_inputs, h)
             run(invert_std, h - 7)
             run(normalise, h - 7)
-            run(add_bias, h - 5)
-            run(minus_mean, h - 5)
-            run(add_src, h - 13)
             run(copy_cat, h - 2)
             run(square_sum, h - 6)
             run(gain_shift, h - 10)

from contextlib import ExitStack

import concourse.mybir as mybir
from concourse.masks import make_identity

F32 = mybir.dt.float32
BF16 = mybir.dt.bfloat16
U32 = mybir.dt.uint32
U8 = mybir.dt.uint8
FP8X4 = mybir.dt.float8_e4m3fn_x4
ALU = mybir.AluOpType
ACT = mybir.ActivationFunctionType

P = 128
ROWS = 512 * 8
D = 512
BLOCKS = D // P
PASSES = 2
HALVES = 2
TILES = ROWS // P
PAIR = 2
PAIR_ROWS = PAIR * P
PAIRS = ROWS // PAIR_ROWS
EPS = 1e-5
ROUNDS_BEFORE_QUANTISING_WEIGHT = 2
LAST_LAG = 13

FLOPS = 2 * ROWS * (PASSES * 512) * D


def tile_stulayer_pb_t_kernel(tc, u, attn_out, src_norm, w_out, b_out, ln2_w, ln2_b, out):
    nc = tc.nc

    def pair_rows(x, j):
        rows = x.flatten_outer_dims()[j * PAIR_ROWS : (j + 1) * PAIR_ROWS, :]
        return rows.rearrange("(p i) d -> p (i d)", i=PAIR)

    def tile_rows(x, m):
        j, i = divmod(m, PAIR)
        return pair_rows(x, j)[:, i * D : (i + 1) * D]

    with ExitStack() as pools:
        const = pools.enter_context(tc.tile_pool(name="const", bufs=1))
        inputs = pools.enter_context(tc.tile_pool(name="inputs", bufs=1))
        two = pools.enter_context(tc.tile_pool(name="two", bufs=2))
        three = pools.enter_context(tc.tile_pool(name="three", bufs=3))
        four = pools.enter_context(tc.tile_pool(name="four", bufs=4))
        six = pools.enter_context(tc.tile_pool(name="six", bufs=6))
        psum = pools.enter_context(tc.psum_pool(name="psum", bufs=2))

        vec_rows = const.tile([P, P], BF16)
        nc.vector.memset(vec_rows[:], 0.0)
        nc.scalar.dma_start(out=vec_rows[0:BLOCKS, :], in_=ln2_w.rearrange("(f p) -> f p", p=P))
        nc.scalar.dma_start(out=vec_rows[BLOCKS : 2 * BLOCKS, :], in_=ln2_b.rearrange("(f p) -> f p", p=P))
        b_row = const.tile([P, D], BF16)
        nc.vector.memset(b_row[:], 0.0)
        nc.scalar.dma_start(out=b_row[0:1, :], in_=b_out.rearrange("(o d) -> o d", o=1))
        w_raw = const.tile([P, PASSES * HALVES, 2 * D], BF16)
        nc.sync.dma_start(
            out=w_raw[:],
            in_=w_out.rearrange("(s q e) n -> q s (e n)", s=PASSES * HALVES, e=2),
        )

        u_sb, a_sb, x_sb = [], [], []
        for j in range(PAIRS):
            u_j = inputs.tile([P, PAIR * D], BF16, name="u%d" % j)
            a_j = inputs.tile([P, PAIR * D], BF16, name="a%d" % j)
            x_j = inputs.tile([P, PAIR * D], BF16, name="x%d" % j)
            nc.sync.dma_start(out=u_j[:], in_=pair_rows(u, j))
            nc.sync.dma_start(out=a_j[:], in_=pair_rows(attn_out, j))
            nc.sync.dma_start(out=x_j[:], in_=pair_rows(src_norm, j))
            u_sb.append(u_j)
            a_sb.append(a_j)
            x_sb.append(x_j)

        ident = const.tile([P, P], F32)
        make_identity(nc, ident[:])
        ones = const.tile([P, P], BF16)
        nc.vector.memset(ones[:], 1.0)
        eps_col = const.tile([P, 1], F32)
        nc.vector.memset(eps_col[:], EPS)
        first_sqrt = const.tile([P, 1], F32)
        nc.scalar.activation(out=first_sqrt[:], in_=eps_col[:], func=ACT.Sqrt)

        w_grouped = const.tile([P, PASSES, D * 4], BF16, align_bytes=64)
        w_codes = const.tile([P, PASSES, D], U32, align_bytes=64)
        w_scales = const.tile([P, PASSES, D], U8, align_bytes=64)
        vec_rows_f32 = const.tile([P, P], F32)
        vec_cols = const.tile([P, 2 * BLOCKS], F32)
        b_bc = const.tile([P, D], F32)

        def regroup_weight():
            for c in range(PASSES):
                rows_of_pass = w_raw[:, c * HALVES : (c + 1) * HALVES, :].rearrange("p h (e n) -> p n (h e)", e=2)
                words_of_pass = w_grouped[:, c, :].rearrange("p (n t) -> p n t", t=4)
                if c == 0:
                    nc.vector.tensor_copy(out=words_of_pass, in_=rows_of_pass)
                else:
                    nc.scalar.copy(out=words_of_pass, in_=rows_of_pass)

        def quantise_weight():
            for c in range(PASSES):
                nc.vector.quantize_mx(
                    out=w_codes[:, c, :].bitcast(FP8X4), scales=w_scales[:, c, :], in_=w_grouped[:, c, :]
                )

        def prepare_gain_shift():
            nc.vector.tensor_copy(out=vec_rows_f32[:], in_=vec_rows[:])
            vec_t = psum.tile([P, D], F32, tag="w_ps")
            nc.tensor.transpose(vec_t[:, 0:P], vec_rows_f32[:], ident[:])
            nc.vector.tensor_copy(out=vec_cols[:], in_=vec_t[:, 0 : 2 * BLOCKS])

        def prepare_bias():
            b_ps = psum.tile([P, D], F32, tag="y_t")
            nc.tensor.matmul(out=b_ps[:], lhsT=ones[:], rhs=b_row[:], start=True, stop=True)
            nc.vector.tensor_copy(out=b_bc[:], in_=b_ps[:])

        res, cat_t, grouped, codes, scales, z, zb, y, y_t, w_t, w_ps, result = {}, {}, {}, {}, {}, {}, {}, {}, {}, {}, {}, {}
        row_sum, neg_mean, sq_sum, std, rstd = {}, {}, {}, {}, {}

        def add_inputs(m):
            j, i = divmod(m, PAIR)
            cols = slice(i * D, (i + 1) * D)
            res[m] = three.tile([P, D], BF16, name="res")
            nc.vector.tensor_tensor(out=res[m][:], in0=u_sb[j][:, cols], in1=a_sb[j][:, cols], op=ALU.add)

        def transpose_cat(m):
            j, i = divmod(m, PAIR)
            cat_words = [res[m][:].bitcast(F32), x_sb[j][:].bitcast(F32)[:, i * (D // 2) : (i + 1) * (D // 2)]]
            cat_t[m] = psum.tile([P, PASSES * HALVES, P], F32, tag="cat_t", name="cat_t")
            for c in range(PASSES):
                for h in range(HALVES):
                    nc.tensor.transpose(
                        cat_t[m][:, c * HALVES + h, :], cat_words[c][:, h * P : (h + 1) * P], ident[:]
                    )

        def copy_cat(m):
            grouped[m] = three.tile([P, PASSES * P * 4], BF16, align_bytes=64, name="grouped")
            nc.scalar.copy(
                out=grouped[m][:].bitcast(F32).rearrange("p (c r h) -> p c r h", c=PASSES, h=HALVES),
                in_=cat_t[m][:].rearrange("p (c h) r -> p c r h", h=HALVES),
            )

        def quantise(m):
            codes[m] = three.tile([P, PASSES * P], U32, align_bytes=64, name="codes")
            scales[m] = three.tile([P, PASSES * P], U8, align_bytes=64, name="scales")
            nc.vector.quantize_mx(out=codes[m][:].bitcast(FP8X4), scales=scales[m][:], in_=grouped[m][:])

        def project(m):
            z[m] = psum.tile([P, D], F32, tag="z", name="z")
            for c in range(PASSES):
                cols = slice(c * P, (c + 1) * P)
                nc.tensor.matmul_mx(
                    out=z[m][:],
                    lhsT=codes[m][:, cols].bitcast(FP8X4),
                    lhsT_scale=scales[m][:, cols],
                    rhs=w_codes[:, c, :].bitcast(FP8X4),
                    rhs_scale=w_scales[:, c, :],
                    start=(c == 0),
                    stop=(c == PASSES - 1),
                )

        def add_bias(m):
            zb[m] = four.tile([P, D], F32, name="zb")
            row_sum[m] = four.tile([P, 1], F32, name="row_sum")
            nc.vector.scalar_tensor_tensor(
                out=zb[m][:], in0=z[m][:], scalar=1.0, in1=b_bc[:], op0=ALU.mult, op1=ALU.add,
                accum_out=row_sum[m][:],
            )

        def minus_mean(m):
            neg_mean[m] = four.tile([P, 1], F32, name="neg_mean")
            nc.gpsimd.tensor_scalar(
                out=neg_mean[m][:], in0=row_sum[m][:], scalar1=-1.0 / D, scalar2=0.0, op0=ALU.mult, op1=ALU.add
            )

        def square_sum(m):
            squares = two.tile([P, D], BF16, name="squares")
            sq_sum[m] = four.tile([P, 1], F32, name="sq_sum")
            nc.scalar.activation(
                out=squares[:], in_=zb[m][:], func=ACT.Square, bias=neg_mean[m][:], scale=1.0, accum_out=sq_sum[m][:]
            )

        def standard_deviation(m):
            std[m] = four.tile([P, 1], F32, name="std")
            nc.scalar.activation(out=std[m][:], in_=sq_sum[m][:], func=ACT.Sqrt, bias=eps_col[:], scale=1.0 / D)

        def invert_std(m):
            rstd[m] = four.tile([P, 1], F32, name="rstd")
            nc.vector.reciprocal(out=rstd[m][:], in_=std[m][:])

        def normalise(m):
            y[m] = six.tile([P, D], F32, name="y")
            nc.gpsimd.tensor_scalar(
                out=y[m][:], in0=zb[m][:], scalar1=neg_mean[m][:], scalar2=rstd[m][:], op0=ALU.add, op1=ALU.mult
            )

        def blocks_of(bank):
            return range(bank * (BLOCKS // PAIR), (bank + 1) * (BLOCKS // PAIR))

        def transpose_y(s):
            j, bank = divmod(s, PAIR)
            y_t[s] = psum.tile([P, BLOCKS // PAIR, PAIR, P], F32, tag="y_t", name="y_t")
            for slot, f in enumerate(blocks_of(bank)):
                for i in range(PAIR):
                    nc.tensor.transpose(y_t[s][:, slot, i, :], y[j * PAIR + i][:, f * P : (f + 1) * P], ident[:])

        def gain_shift(s):
            j, bank = divmod(s, PAIR)
            if bank == 0:
                w_t[j] = three.tile([P, BLOCKS, PAIR, P], F32, name="w_t")
            for slot, f in enumerate(blocks_of(bank)):
                nc.scalar.activation(
                    out=w_t[j][:, f, :, :], in_=y_t[s][:, slot, :, :], func=ACT.Identity,
                    scale=vec_cols[:, f : f + 1], bias=vec_cols[:, BLOCKS + f : BLOCKS + f + 1],
                )

        def transpose_back(m):
            j, i = divmod(m, PAIR)
            w_ps[m] = psum.tile([P, D], F32, tag="w_ps", name="w_ps")
            for f in range(BLOCKS):
                nc.tensor.transpose(w_ps[m][:, f * P : (f + 1) * P], w_t[j][:, f, i, :], ident[:])

        def add_src(m):
            j, i = divmod(m, PAIR)
            result[m] = four.tile([P, D], F32, name="result")
            nc.vector.tensor_tensor(
                out=result[m][:], in0=w_ps[m][:], in1=x_sb[j][:, i * D : (i + 1) * D], op=ALU.add
            )
            nc.sync.dma_start(out=tile_rows(out, m), in_=result[m][:])

        def run(stage, m):
            if 0 <= m < TILES:
                stage(m)

        def one_round(h):
            run(add_bias, h - 5)
            run(minus_mean, h - 5)
            run(quantise, h - 3)
            run(add_src, h - 13)
            run(add_inputs, h)
            run(invert_std, h - 7)
            run(normalise, h - 7)
            run(copy_cat, h - 2)
            run(square_sum, h - 6)
            run(gain_shift, h - 10)
            run(standard_deviation, h - 6)
            run(transpose_back, h - 12)
            run(transpose_y, h - 9)
            run(transpose_cat, h - 1)
            run(project, h - 4)

        with tc.manual_schedule():
            regroup_weight()
            for h in range(ROUNDS_BEFORE_QUANTISING_WEIGHT):
                one_round(h)
            quantise_weight()
            prepare_bias()
            prepare_gain_shift()
            for h in range(ROUNDS_BEFORE_QUANTISING_WEIGHT, TILES + LAST_LAG + 1):
                one_round(h)
